import numpy as np
import ml_dtypes

BF16 = ml_dtypes.bfloat16


def bf(x):
    return np.asarray(x, np.float32).astype(BF16)


def f32(x):
    return np.asarray(x, np.float32)


def f64(x):
    return np.asarray(x).astype(np.float64)


def striped(idx):
    return np.tile(idx.reshape(-1, 16).T, (8, 1))


C, S, N = 128, 4096, 1024
EPS = 1e-5


def setup_inputs():
    return {"base": f32(np.random.standard_normal((C, S))), "x": f32(np.random.standard_normal((C, N))), "bo": f32(0.1 * np.random.standard_normal((C, 1))), "gain": f32(1.0 + 0.1 * np.random.standard_normal((C, 1))), "beta": f32(0.1 * np.random.standard_normal((C, 1))), "offs": striped(np.random.permutation(S)[:N])}


def reference(base, x, bo, gain, beta, offs):
    idx = offs[:16].T.reshape(-1)
    r = f64(x) + f64(bo)
    mu = r.mean(0, keepdims=True)
    var = ((r - mu) ** 2).mean(0, keepdims=True)
    res = f64(base).copy()
    res[:, idx] = (r - mu) / np.sqrt(var + EPS) * f64(gain) + f64(beta)
    return res

@@ -1,0 +1,73 @@
+import concourse.masks as masks
+import concourse.mybir as mybir
+
+F32 = mybir.dt.float32
+U16 = mybir.dt.uint16
+ALU = mybir.AluOpType
+ACT = mybir.ActivationFunctionType
+
+C = 128
+S = 4096
+N = 1024
+EPS = 1e-5
+BANK = 512
+
+FLOPS = 9 * C * N
+BYTES = 4 * (C * S + C * (S - N) + C * N + 3 * C) + 2 * N
+
+
+def tile_p2pdecoderlayer_kernel(tc, base, x, bo, gain, beta, offs, out):
+    nc = tc.nc
+    with (
+        tc.tile_pool(name="held", bufs=1) as held,
+        tc.psum_pool(name="psum", bufs=1) as psum,
+    ):
+        x_sb = held.tile([C, N], F32, name="x_sb")
+        nc.sync.dma_start(x_sb[:], x)
+        offsets = held.tile([C, N // 16], U16, name="offsets")
+        nc.sync.dma_start(offsets[:], offs)
+        window = held.tile([C, S], F32, name="window")
+        nc.sync.dma_start(window[:], base)
+        bo_sb = held.tile([C, 1], F32, name="bo_sb")
+        nc.scalar.dma_start(bo_sb[:], bo)
+        gain_sb = held.tile([C, 1], F32, name="gain_sb")
+        nc.scalar.dma_start(gain_sb[:], gain)
+        beta_sb = held.tile([C, 1], F32, name="beta_sb")
+        nc.scalar.dma_start(beta_sb[:], beta)
+
+        identity = held.tile([C, C], F32, name="identity")
+        masks.make_identity(nc, identity[:])
+        centre = held.tile([C, C], F32, name="centre")
+        nc.vector.tensor_scalar_add(centre[:], identity[:], -1.0 / C)
+        average = held.tile([C, C], F32, name="average")
+        nc.gpsimd.memset(average[:], 1.0 / C)
+        eps_sb = held.tile([C, 1], F32, name="eps_sb")
+        nc.gpsimd.memset(eps_sb[:], EPS)
+
+        r = held.tile([C, N], F32, name="r")
+        sq = held.tile([C, N], F32, name="sq")
+        rstd = held.tile([C, N], F32, name="rstd")
+        scaled = held.tile([C, N], F32, name="scaled")
+        banks = range(N // BANK)
+        centred = [psum.tile([C, BANK], F32, name=f"centred{b}") for b in banks]
+        var = [psum.tile([C, BANK], F32, name=f"var{b}") for b in banks]
+
+        for b in banks:
+            cols = slice(b * BANK, (b + 1) * BANK)
+            nc.vector.tensor_scalar_add(r[:, cols], x_sb[:, cols], bo_sb[:])
+            nc.tensor.matmul(centred[b][:], centre[:], r[:, cols], start=True, stop=True)
+            nc.scalar.activation(sq[:, cols], centred[b][:], ACT.Square)
+
+        beta_wide = held.tile([C, N], F32, name="beta_wide")
+        nc.vector.tensor_copy(beta_wide[:], beta_sb[:].to_broadcast([C, N]))
+
+        for b in banks:
+            cols = slice(b * BANK, (b + 1) * BANK)
+            nc.tensor.matmul(var[b][:], average[:], sq[:, cols], start=True, stop=True)
+            nc.scalar.activation(rstd[:, cols], var[b][:], ACT.Abs_reciprocal_sqrt, bias=eps_sb[:])
+            nc.vector.scalar_tensor_tensor(
+                scaled[:, cols], centred[b][:], gain_sb[:], rstd[:, cols], ALU.mult, ALU.mult
+            )
+
+        nc.vector.tensor_tensor(window[:].indirect(offsets[:]), scaled[:], beta_wide[:], ALU.add)
+        nc.sync.dma_start(out, window[:])

@@ -10,63 +10,86 @@ C = 128
 S = 4096
 N = 1024
 EPS = 1e-5
-BANK = 512
 
 FLOPS = 9 * C * N
 BYTES = 4 * (C * S + C * (S - N) + C * N + 3 * C) + 2 * N
+
+PIECE = 256
+PIECES = N // PIECE
+WARM_UP = 4
 
 
 def tile_p2pdecoderlayer_kernel(tc, base, x, bo, gain, beta, offs, out):
     nc = tc.nc
     with (
         tc.tile_pool(name="held", bufs=1) as held,
-        tc.psum_pool(name="psum", bufs=1) as psum,
+        tc.psum_pool(name="psum_centred", bufs=PIECES) as psum_centred,
+        tc.psum_pool(name="psum_other", bufs=4) as psum_other,
     ):
         x_sb = held.tile([C, N], F32, name="x_sb")
-        nc.sync.dma_start(x_sb[:], x)
-        offsets = held.tile([C, N // 16], U16, name="offsets")
-        nc.sync.dma_start(offsets[:], offs)
+        nc.sync.dma_start(x_sb[:, 0 : N // 2], x[:, 0 : N // 2])
+        nc.sync.dma_start(x_sb[:, N // 2 : N], x[:, N // 2 : N])
         window = held.tile([C, S], F32, name="window")
         nc.sync.dma_start(window[:], base)
-        bo_sb = held.tile([C, 1], F32, name="bo_sb")
-        nc.scalar.dma_start(bo_sb[:], bo)
-        gain_sb = held.tile([C, 1], F32, name="gain_sb")
-        nc.scalar.dma_start(gain_sb[:], gain)
-        beta_sb = held.tile([C, 1], F32, name="beta_sb")
-        nc.scalar.dma_start(beta_sb[:], beta)
+        offsets = held.tile([C, N // 16], U16, name="offsets")
+        nc.sync.dma_start(offsets[:], offs)
+        rows = held.tile([3, C], F32, name="rows")
+        for k, vector in enumerate((bo, gain, beta)):
+            nc.scalar.dma_start(rows[k : k + 1, :], vector.rearrange("c one -> one c"))
 
-        identity = held.tile([C, C], F32, name="identity")
-        masks.make_identity(nc, identity[:])
-        centre = held.tile([C, C], F32, name="centre")
-        nc.vector.tensor_scalar_add(centre[:], identity[:], -1.0 / C)
         average = held.tile([C, C], F32, name="average")
-        nc.gpsimd.memset(average[:], 1.0 / C)
+        nc.vector.memset(average[:], 1.0 / C)
         eps_sb = held.tile([C, 1], F32, name="eps_sb")
-        nc.gpsimd.memset(eps_sb[:], EPS)
+        nc.vector.memset(eps_sb[:], EPS)
+        identity3 = held.tile([3, 3], F32, name="identity3")
+        masks.make_identity(nc, identity3[:])
+        centre = held.tile([C, C], F32, name="centre")
+        nc.gpsimd.memset(centre[:], -1.0 / C)
+        nc.gpsimd.affine_select(
+            out=centre[:],
+            in_=centre[:],
+            compare_op=ALU.not_equal,
+            fill=1.0 - 1.0 / C,
+            base=0,
+            pattern=[[-1, C]],
+            channel_multiplier=1,
+        )
+
+        table_warm = held.tile([C, 1], F32, name="table_warm")
+        nc.scalar.activation(table_warm[:], eps_sb[:], ACT.Abs_reciprocal_sqrt)
+        clock_warm = psum_other.tile([C, C], F32, name="clock_warm", tag="other")
+        for repeat in range(WARM_UP):
+            nc.tensor.matmul(clock_warm[:], average[:], average[:], start=True, stop=True)
+
+        columns_ps = psum_other.tile([C, 3], F32, name="columns_ps", tag="other")
+        nc.tensor.matmul(columns_ps[:], rows[:], identity3[:], start=True, stop=True)
+        columns = held.tile([C, 3], F32, name="columns")
+        nc.vector.tensor_copy(columns[:], columns_ps[:])
+        bo_sb, gain_sb, beta_sb = columns[:, 0:1], columns[:, 1:2], columns[:, 2:3]
+        beta_wide = held.tile([C, N], F32, name="beta_wide")
+        nc.gpsimd.tensor_copy(beta_wide[:], beta_sb.to_broadcast([C, N]))
 
         r = held.tile([C, N], F32, name="r")
         sq = held.tile([C, N], F32, name="sq")
         rstd = held.tile([C, N], F32, name="rstd")
         scaled = held.tile([C, N], F32, name="scaled")
-        banks = range(N // BANK)
-        centred = [psum.tile([C, BANK], F32, name=f"centred{b}") for b in banks]
-        var = [psum.tile([C, BANK], F32, name=f"var{b}") for b in banks]
 
-        for b in banks:
-            cols = slice(b * BANK, (b + 1) * BANK)
-            nc.vector.tensor_scalar_add(r[:, cols], x_sb[:, cols], bo_sb[:])
-            nc.tensor.matmul(centred[b][:], centre[:], r[:, cols], start=True, stop=True)
-            nc.scalar.activation(sq[:, cols], centred[b][:], ACT.Square)
+        centred = []
+        for p in range(PIECES):
+            cols = slice(p * PIECE, (p + 1) * PIECE)
+            nc.vector.tensor_scalar_add(r[:, cols], x_sb[:, cols], bo_sb)
+            centred_p = psum_centred.tile([C, PIECE], F32, name="centred_p")
+            nc.tensor.matmul(centred_p[:], centre[:], r[:, cols], start=True, stop=True)
+            nc.scalar.activation(sq[:, cols], centred_p[:], ACT.Square)
+            centred.append(centred_p)
 
-        beta_wide = held.tile([C, N], F32, name="beta_wide")
-        nc.vector.tensor_copy(beta_wide[:], beta_sb[:].to_broadcast([C, N]))
-
-        for b in banks:
-            cols = slice(b * BANK, (b + 1) * BANK)
-            nc.tensor.matmul(var[b][:], average[:], sq[:, cols], start=True, stop=True)
-            nc.scalar.activation(rstd[:, cols], var[b][:], ACT.Abs_reciprocal_sqrt, bias=eps_sb[:])
+        for p in range(PIECES):
+            cols = slice(p * PIECE, (p + 1) * PIECE)
+            var_p = psum_other.tile([C, PIECE], F32, name="var_p", tag="other")
+            nc.tensor.matmul(var_p[:], average[:], sq[:, cols], start=True, stop=True)
+            nc.scalar.activation(rstd[:, cols], var_p[:], ACT.Abs_reciprocal_sqrt, bias=eps_sb[:])
             nc.vector.scalar_tensor_tensor(
-                scaled[:, cols], centred[b][:], gain_sb[:], rstd[:, cols], ALU.mult, ALU.mult
+                scaled[:, cols], centred[p][:], gain_sb, rstd[:, cols], ALU.mult, ALU.mult
             )
 
         nc.vector.tensor_tensor(window[:].indirect(offsets[:]), scaled[:], beta_wide[:], ALU.add)

@@ -16,7 +16,7 @@ BYTES = 4 * (C * S + C * (S - N) + C * N + 3 * C) + 2 * N
 
 PIECE = 256
 PIECES = N // PIECE
-WARM_UP = 4
+WARM_UP = 3
 
 
 def tile_p2pdecoderlayer_kernel(tc, base, x, bo, gain, beta, offs, out):
@@ -27,22 +27,22 @@ def tile_p2pdecoderlayer_kernel(tc, base, x, bo, gain, beta, offs, out):
         tc.psum_pool(name="psum_other", bufs=4) as psum_other,
     ):
         x_sb = held.tile([C, N], F32, name="x_sb")
-        nc.sync.dma_start(x_sb[:, 0 : N // 2], x[:, 0 : N // 2])
-        nc.sync.dma_start(x_sb[:, N // 2 : N], x[:, N // 2 : N])
-        window = held.tile([C, S], F32, name="window")
-        nc.sync.dma_start(window[:], base)
         offsets = held.tile([C, N // 16], U16, name="offsets")
+        window = held.tile([C, S], F32, name="window")
+        bo_sb = held.tile([C, 1], F32, name="bo_sb")
+        gain_sb = held.tile([C, 1], F32, name="gain_sb")
+        beta_sb = held.tile([C, 1], F32, name="beta_sb")
+        nc.sync.dma_start(x_sb[:, 0 : N // 2], x[:, 0 : N // 2])
+        nc.scalar.dma_start(bo_sb[:], bo)
+        nc.sync.dma_start(x_sb[:, N // 2 : N], x[:, N // 2 : N])
+        nc.scalar.dma_start(gain_sb[:], gain)
         nc.sync.dma_start(offsets[:], offs)
-        rows = held.tile([3, C], F32, name="rows")
-        for k, vector in enumerate((bo, gain, beta)):
-            nc.scalar.dma_start(rows[k : k + 1, :], vector.rearrange("c one -> one c"))
+        nc.scalar.dma_start(beta_sb[:], beta)
+        nc.sync.dma_start(window[:, 0 : S // 2], base[:, 0 : S // 2])
+        nc.scalar.dma_start(window[:, S // 2 : S], base[:, S // 2 : S])
 
         average = held.tile([C, C], F32, name="average")
-        nc.vector.memset(average[:], 1.0 / C)
-        eps_sb = held.tile([C, 1], F32, name="eps_sb")
-        nc.vector.memset(eps_sb[:], EPS)
-        identity3 = held.tile([3, 3], F32, name="identity3")
-        masks.make_identity(nc, identity3[:])
+        nc.gpsimd.memset(average[:], 1.0 / C)
         centre = held.tile([C, C], F32, name="centre")
         nc.gpsimd.memset(centre[:], -1.0 / C)
         nc.gpsimd.affine_select(
@@ -54,6 +54,8 @@ def tile_p2pdecoderlayer_kernel(tc, base, x, bo, gain, beta, offs, out):
             pattern=[[-1, C]],
             channel_multiplier=1,
         )
+        eps_sb = held.tile([C, 1], F32, name="eps_sb")
+        nc.vector.memset(eps_sb[:], EPS)
 
         table_warm = held.tile([C, 1], F32, name="table_warm")
         nc.scalar.activation(table_warm[:], eps_sb[:], ACT.Abs_reciprocal_sqrt)
@@ -61,36 +63,34 @@ def tile_p2pdecoderlayer_kernel(tc, base, x, bo, gain, beta, offs, out):
         for repeat in range(WARM_UP):
             nc.tensor.matmul(clock_warm[:], average[:], average[:], start=True, stop=True)
 
-        columns_ps = psum_other.tile([C, 3], F32, name="columns_ps", tag="other")
-        nc.tensor.matmul(columns_ps[:], rows[:], identity3[:], start=True, stop=True)
-        columns = held.tile([C, 3], F32, name="columns")
-        nc.vector.tensor_copy(columns[:], columns_ps[:])
-        bo_sb, gain_sb, beta_sb = columns[:, 0:1], columns[:, 1:2], columns[:, 2:3]
         beta_wide = held.tile([C, N], F32, name="beta_wide")
-        nc.gpsimd.tensor_copy(beta_wide[:], beta_sb.to_broadcast([C, N]))
+        nc.gpsimd.tensor_copy(beta_wide[:], beta_sb[:].to_broadcast([C, N]))
 
-        r = held.tile([C, N], F32, name="r")
         sq = held.tile([C, N], F32, name="sq")
+        gained = held.tile([C, N], F32, name="gained")
         rstd = held.tile([C, N], F32, name="rstd")
         scaled = held.tile([C, N], F32, name="scaled")
+        bo_centred = held.tile([C, 1], F32, name="bo_centred")
 
-        centred = []
         for p in range(PIECES):
             cols = slice(p * PIECE, (p + 1) * PIECE)
-            nc.vector.tensor_scalar_add(r[:, cols], x_sb[:, cols], bo_sb)
-            centred_p = psum_centred.tile([C, PIECE], F32, name="centred_p")
-            nc.tensor.matmul(centred_p[:], centre[:], r[:, cols], start=True, stop=True)
-            nc.scalar.activation(sq[:, cols], centred_p[:], ACT.Square)
-            centred.append(centred_p)
+            x_centred = psum_centred.tile([C, PIECE], F32, name="x_centred")
+            nc.tensor.matmul(x_centred[:], centre[:], x_sb[:, cols], start=True, stop=True)
+            if p == 0:
+                bo_centred_ps = psum_other.tile([C, 1], F32, name="bo_centred_ps", tag="other")
+                nc.tensor.matmul(bo_centred_ps[:], centre[:], bo_sb[:], start=True, stop=True)
+                nc.vector.tensor_copy(bo_centred[:], bo_centred_ps[:])
+            nc.scalar.activation(sq[:, cols], x_centred[:], ACT.Square, bias=bo_centred[:])
+            nc.vector.tensor_scalar(
+                gained[:, cols], x_centred[:], bo_centred[:], gain_sb[:], ALU.add, ALU.mult
+            )
 
         for p in range(PIECES):
             cols = slice(p * PIECE, (p + 1) * PIECE)
             var_p = psum_other.tile([C, PIECE], F32, name="var_p", tag="other")
             nc.tensor.matmul(var_p[:], average[:], sq[:, cols], start=True, stop=True)
             nc.scalar.activation(rstd[:, cols], var_p[:], ACT.Abs_reciprocal_sqrt, bias=eps_sb[:])
-            nc.vector.scalar_tensor_tensor(
-                scaled[:, cols], centred[p][:], gain_sb, rstd[:, cols], ALU.mult, ALU.mult
-            )
+            nc.vector.tensor_tensor(scaled[:, cols], gained[:, cols], rstd[:, cols], ALU.mult)
 
         nc.vector.tensor_tensor(window[:].indirect(offsets[:]), scaled[:], beta_wide[:], ALU.add)
         nc.sync.dma_start(out, window[:])

@@ -32,14 +32,14 @@ def tile_p2pdecoderlayer_kernel(tc, base, x, bo, gain, beta, offs, out):
         bo_sb = held.tile([C, 1], F32, name="bo_sb")
         gain_sb = held.tile([C, 1], F32, name="gain_sb")
         beta_sb = held.tile([C, 1], F32, name="beta_sb")
-        nc.sync.dma_start(x_sb[:, 0 : N // 2], x[:, 0 : N // 2])
-        nc.scalar.dma_start(bo_sb[:], bo)
-        nc.sync.dma_start(x_sb[:, N // 2 : N], x[:, N // 2 : N])
-        nc.scalar.dma_start(gain_sb[:], gain)
+        for p in range(PIECES):
+            cols = slice(p * PIECE, (p + 1) * PIECE)
+            nc.sync.dma_start(x_sb[:, cols], x[:, cols])
+        nc.sync.dma_start(window[:], base)
         nc.sync.dma_start(offsets[:], offs)
+        nc.scalar.dma_start(bo_sb[:], bo)
+        nc.scalar.dma_start(gain_sb[:], gain)
         nc.scalar.dma_start(beta_sb[:], beta)
-        nc.sync.dma_start(window[:, 0 : S // 2], base[:, 0 : S // 2])
-        nc.scalar.dma_start(window[:, S // 2 : S], base[:, S // 2 : S])
 
         average = held.tile([C, C], F32, name="average")
         nc.gpsimd.memset(average[:], 1.0 / C)

@@ -35,8 +35,8 @@ def tile_p2pdecoderlayer_kernel(tc, base, x, bo, gain, beta, offs, out):
         for p in range(PIECES):
             cols = slice(p * PIECE, (p + 1) * PIECE)
             nc.sync.dma_start(x_sb[:, cols], x[:, cols])
-        nc.sync.dma_start(window[:], base)
         nc.sync.dma_start(offsets[:], offs)
+        nc.sync.dma_start(window[:], base)
         nc.scalar.dma_start(bo_sb[:], bo)
         nc.scalar.dma_start(gain_sb[:], gain)
         nc.scalar.dma_start(beta_sb[:], beta)

@@ -16,6 +16,7 @@ BYTES = 4 * (C * S + C * (S - N) + C * N + 3 * C) + 2 * N
 
 PIECE = 256
 PIECES = N // PIECE
+LEAD = 8
 WARM_UP = 3
 
 
@@ -26,18 +27,17 @@ def tile_p2pdecoderlayer_kernel(tc, base, x, bo, gain, beta, offs, out):
         tc.psum_pool(name="psum_centred", bufs=PIECES) as psum_centred,
         tc.psum_pool(name="psum_other", bufs=4) as psum_other,
     ):
-        x_sb = held.tile([C, N], F32, name="x_sb")
+        x_sb = held.tile([C, LEAD + N], F32, name="x_sb")
         offsets = held.tile([C, N // 16], U16, name="offsets")
         window = held.tile([C, S], F32, name="window")
-        bo_sb = held.tile([C, 1], F32, name="bo_sb")
         gain_sb = held.tile([C, 1], F32, name="gain_sb")
         beta_sb = held.tile([C, 1], F32, name="beta_sb")
         for p in range(PIECES):
             cols = slice(p * PIECE, (p + 1) * PIECE)
-            nc.sync.dma_start(x_sb[:, cols], x[:, cols])
+            nc.sync.dma_start(x_sb[:, LEAD + p * PIECE : LEAD + (p + 1) * PIECE], x[:, cols])
         nc.sync.dma_start(offsets[:], offs)
         nc.sync.dma_start(window[:], base)
-        nc.scalar.dma_start(bo_sb[:], bo)
+        nc.scalar.dma_start(x_sb[:, LEAD - 1 : LEAD], bo)
         nc.scalar.dma_start(gain_sb[:], gain)
         nc.scalar.dma_start(beta_sb[:], beta)
 
@@ -74,20 +74,27 @@ def tile_p2pdecoderlayer_kernel(tc, base, x, bo, gain, beta, offs, out):
 
         for p in range(PIECES):
             cols = slice(p * PIECE, (p + 1) * PIECE)
-            x_centred = psum_centred.tile([C, PIECE], F32, name="x_centred")
-            nc.tensor.matmul(x_centred[:], centre[:], x_sb[:, cols], start=True, stop=True)
+            extra = 1 if p == 0 else 0
+            product = psum_centred.tile([C, extra + PIECE], F32, name="product")
+            nc.tensor.matmul(
+                product[:],
+                centre[:],
+                x_sb[:, LEAD + p * PIECE - extra : LEAD + (p + 1) * PIECE],
+                start=True,
+                stop=True,
+            )
             if p == 0:
-                bo_centred_ps = psum_other.tile([C, 1], F32, name="bo_centred_ps", tag="other")
-                nc.tensor.matmul(bo_centred_ps[:], centre[:], bo_sb[:], start=True, stop=True)
-                nc.vector.tensor_copy(bo_centred[:], bo_centred_ps[:])
-            nc.scalar.activation(sq[:, cols], x_centred[:], ACT.Square, bias=bo_centred[:])
+                nc.vector.tensor_copy(bo_centred[:], product[:, 0:1])
+            x_centred = product[:, extra:]
+            nc.scalar.activation(sq[:, cols], x_centred, ACT.Square, bias=bo_centred[:])
             nc.vector.tensor_scalar(
-                gained[:, cols], x_centred[:], bo_centred[:], gain_sb[:], ALU.add, ALU.mult
+                gained[:, cols], x_centred, bo_centred[:], gain_sb[:], ALU.add, ALU.mult
             )
 
-        for p in range(PIECES):
-            cols = slice(p * PIECE, (p + 1) * PIECE)
-            var_p = psum_other.tile([C, PIECE], F32, name="var_p", tag="other")
+        starts = [p * PIECE for p in range(PIECES)] + [N - PIECE // 2]
+        for first, end in zip(starts, starts[1:] + [N]):
+            cols = slice(first, end)
+            var_p = psum_other.tile([C, end - first], F32, name="var_p", tag="other")
             nc.tensor.matmul(var_p[:], average[:], sq[:, cols], start=True, stop=True)
             nc.scalar.activation(rstd[:, cols], var_p[:], ACT.Abs_reciprocal_sqrt, bias=eps_sb[:])
             nc.vector.tensor_tensor(scaled[:, cols], gained[:, cols], rstd[:, cols], ALU.mult)

@@ -2,6 +2,7 @@ import concourse.masks as masks
 import concourse.mybir as mybir
 
 F32 = mybir.dt.float32
+BF16 = mybir.dt.bfloat16
 U16 = mybir.dt.uint16
 ALU = mybir.AluOpType
 ACT = mybir.ActivationFunctionType
@@ -17,7 +18,8 @@ BYTES = 4 * (C * S + C * (S - N) + C * N + 3 * C) + 2 * N
 PIECE = 256
 PIECES = N // PIECE
 LEAD = 8
-WARM_UP = 3
+WARM_UP = 4
+BANK = 512
 
 
 def tile_p2pdecoderlayer_kernel(tc, base, x, bo, gain, beta, offs, out):
@@ -27,6 +29,9 @@ def tile_p2pdecoderlayer_kernel(tc, base, x, bo, gain, beta, offs, out):
         tc.psum_pool(name="psum_centred", bufs=PIECES) as psum_centred,
         tc.psum_pool(name="psum_other", bufs=4) as psum_other,
     ):
+        spark = held.tile([C, 2], BF16, name="spark")
+        nc.gpsimd.memset(spark[:], 1.0)
+
         x_sb = held.tile([C, LEAD + N], F32, name="x_sb")
         offsets = held.tile([C, N // 16], U16, name="offsets")
         window = held.tile([C, S], F32, name="window")
@@ -59,9 +64,15 @@ def tile_p2pdecoderlayer_kernel(tc, base, x, bo, gain, beta, offs, out):
 
         table_warm = held.tile([C, 1], F32, name="table_warm")
         nc.scalar.activation(table_warm[:], eps_sb[:], ACT.Abs_reciprocal_sqrt)
-        clock_warm = psum_other.tile([C, C], F32, name="clock_warm", tag="other")
+        clock_warm = psum_other.tile([C, BANK], F32, name="clock_warm", tag="other")
         for repeat in range(WARM_UP):
-            nc.tensor.matmul(clock_warm[:], average[:], average[:], start=True, stop=True)
+            nc.tensor.matmul(
+                clock_warm[:],
+                spark[:, 0:1].to_broadcast([C, C]),
+                spark[:, 0:1].to_broadcast([C, BANK]),
+                start=True,
+                stop=True,
+            )
 
         beta_wide = held.tile([C, N], F32, name="beta_wide")
         nc.gpsimd.tensor_copy(beta_wide[:], beta_sb[:].to_broadcast([C, N]))

@@ -75,7 +75,7 @@ def tile_p2pdecoderlayer_kernel(tc, base, x, bo, gain, beta, offs, out):
             )
 
         beta_wide = held.tile([C, N], F32, name="beta_wide")
-        nc.gpsimd.tensor_copy(beta_wide[:], beta_sb[:].to_broadcast([C, N]))
+        nc.vector.tensor_copy(beta_wide[:], beta_sb[:].to_broadcast([C, N]))
 
         sq = held.tile([C, N], F32, name="sq")
         gained = held.tile([C, N], F32, name="gained")

@@ -18,6 +18,9 @@ BYTES = 4 * (C * S + C * (S - N) + C * N + 3 * C) + 2 * N
 PIECE = 256
 PIECES = N // PIECE
 LEAD = 8
+TURNED = 1
+BLOCK = 128
+BLOCKS = PIECE // BLOCK
 WARM_UP = 4
 BANK = 512
 
@@ -26,7 +29,8 @@ def tile_p2pdecoderlayer_kernel(tc, base, x, bo, gain, beta, offs, out):
     nc = tc.nc
     with (
         tc.tile_pool(name="held", bufs=1) as held,
-        tc.psum_pool(name="psum_centred", bufs=PIECES) as psum_centred,
+        tc.psum_pool(name="psum_centred", bufs=PIECES - 1) as psum_centred,
+        tc.psum_pool(name="psum_turned", bufs=1) as psum_turned,
         tc.psum_pool(name="psum_other", bufs=4) as psum_other,
     ):
         spark = held.tile([C, 2], BF16, name="spark")
@@ -37,17 +41,14 @@ def tile_p2pdecoderlayer_kernel(tc, base, x, bo, gain, beta, offs, out):
         window = held.tile([C, S], F32, name="window")
         gain_sb = held.tile([C, 1], F32, name="gain_sb")
         beta_sb = held.tile([C, 1], F32, name="beta_sb")
-        for p in range(PIECES):
-            cols = slice(p * PIECE, (p + 1) * PIECE)
-            nc.sync.dma_start(x_sb[:, LEAD + p * PIECE : LEAD + (p + 1) * PIECE], x[:, cols])
+        for first, end in ((0, PIECE), (PIECE, 2 * PIECE), (2 * PIECE, N)):
+            nc.sync.dma_start(x_sb[:, LEAD + first : LEAD + end], x[:, first:end])
         nc.sync.dma_start(offsets[:], offs)
         nc.sync.dma_start(window[:], base)
         nc.scalar.dma_start(x_sb[:, LEAD - 1 : LEAD], bo)
         nc.scalar.dma_start(gain_sb[:], gain)
         nc.scalar.dma_start(beta_sb[:], beta)
 
-        average = held.tile([C, C], F32, name="average")
-        nc.gpsimd.memset(average[:], 1.0 / C)
         centre = held.tile([C, C], F32, name="centre")
         nc.gpsimd.memset(centre[:], -1.0 / C)
         nc.gpsimd.affine_select(
@@ -59,6 +60,10 @@ def tile_p2pdecoderlayer_kernel(tc, base, x, bo, gain, beta, offs, out):
             pattern=[[-1, C]],
             channel_multiplier=1,
         )
+        identity = held.tile([C, C], F32, name="identity")
+        masks.make_identity(nc, identity[:])
+        average = held.tile([C, C], F32, name="average")
+        nc.gpsimd.memset(average[:], 1.0 / C)
         eps_sb = held.tile([C, 1], F32, name="eps_sb")
         nc.vector.memset(eps_sb[:], EPS)
 
@@ -83,8 +88,14 @@ def tile_p2pdecoderlayer_kernel(tc, base, x, bo, gain, beta, offs, out):
         scaled = held.tile([C, N], F32, name="scaled")
         bo_centred = held.tile([C, 1], F32, name="bo_centred")
 
-        for p in range(PIECES):
-            cols = slice(p * PIECE, (p + 1) * PIECE)
+        r = held.tile([C, PIECE], F32, name="r")
+        stats = held.tile([C, BLOCKS, 6], F32, name="stats")
+        moments = held.tile([C, BLOCKS, 2], F32, name="moments")
+        rstd_token = held.tile([C, BLOCKS], F32, name="rstd_token")
+        normal = held.tile([C, PIECE], F32, name="normal")
+        blocks = [slice(b * BLOCK, (b + 1) * BLOCK) for b in range(BLOCKS)]
+
+        def centred(p):
             extra = 1 if p == 0 else 0
             product = psum_centred.tile([C, extra + PIECE], F32, name="product")
             nc.tensor.matmul(
@@ -96,19 +107,69 @@ def tile_p2pdecoderlayer_kernel(tc, base, x, bo, gain, beta, offs, out):
             )
             if p == 0:
                 nc.vector.tensor_copy(bo_centred[:], product[:, 0:1])
-            x_centred = product[:, extra:]
+            return product[:, extra:]
+
+        def squared_and_gained(p, x_centred):
+            cols = slice(p * PIECE, (p + 1) * PIECE)
             nc.scalar.activation(sq[:, cols], x_centred, ACT.Square, bias=bo_centred[:])
             nc.vector.tensor_scalar(
                 gained[:, cols], x_centred, bo_centred[:], gain_sb[:], ALU.add, ALU.mult
             )
 
-        starts = [p * PIECE for p in range(PIECES)] + [N - PIECE // 2]
-        for first, end in zip(starts, starts[1:] + [N]):
+        def normalised(first, end):
             cols = slice(first, end)
             var_p = psum_other.tile([C, end - first], F32, name="var_p", tag="other")
             nc.tensor.matmul(var_p[:], average[:], sq[:, cols], start=True, stop=True)
             nc.scalar.activation(rstd[:, cols], var_p[:], ACT.Abs_reciprocal_sqrt, bias=eps_sb[:])
             nc.vector.tensor_tensor(scaled[:, cols], gained[:, cols], rstd[:, cols], ALU.mult)
+
+        def turned():
+            nc.scalar.activation(
+                r[:],
+                x_sb[:, LEAD + TURNED * PIECE : LEAD + (TURNED + 1) * PIECE],
+                ACT.Identity,
+                bias=x_sb[:, LEAD - 1 : LEAD],
+            )
+            by_token = psum_turned.tile([C, PIECE], F32, name="by_token", tag="turned")
+            for block in blocks:
+                nc.tensor.transpose(by_token[:, block], r[:, block], identity[:])
+            return by_token
+
+        def normalised_by_token(by_token):
+            for b, block in enumerate(blocks):
+                nc.vector.bn_stats(stats[:, b, :], by_token[:, block])
+                nc.vector.bn_aggr(moments[:, b, :], stats[:, b, :])
+            nc.scalar.activation(rstd_token[:], moments[:, :, 1], ACT.Abs_reciprocal_sqrt, bias=eps_sb[:])
+            for b, block in enumerate(blocks):
+                nc.vector.tensor_scalar(
+                    normal[:, block],
+                    by_token[:, block],
+                    moments[:, b, 0:1],
+                    rstd_token[:, b : b + 1],
+                    ALU.subtract,
+                    ALU.mult,
+                )
+
+        def turned_back():
+            by_channel = psum_turned.tile([C, PIECE], F32, name="by_channel", tag="turned")
+            for block in blocks:
+                nc.tensor.transpose(by_channel[:, block], normal[:, block], identity[:])
+            nc.scalar.activation(
+                scaled[:, TURNED * PIECE : (TURNED + 1) * PIECE], by_channel[:], ACT.Identity, scale=gain_sb[:]
+            )
+
+        first_piece, second_piece, last_piece = [p for p in range(PIECES) if p != TURNED]
+        x_centred = centred(first_piece)
+        by_token = turned()
+        squared_and_gained(first_piece, x_centred)
+        normalised_by_token(by_token)
+        squared_and_gained(second_piece, centred(second_piece))
+        squared_and_gained(last_piece, centred(last_piece))
+        normalised(first_piece * PIECE, (first_piece + 1) * PIECE)
+        normalised(second_piece * PIECE, (second_piece + 1) * PIECE)
+        turned_back()
+        normalised(N - PIECE, N - PIECE // 2)
+        normalised(N - PIECE // 2, N)
 
         nc.vector.tensor_tensor(window[:].indirect(offsets[:]), scaled[:], beta_wide[:], ALU.add)
         nc.sync.dma_start(out, window[:])

@@ -36,7 +36,7 @@ def tile_p2pdecoderlayer_kernel(tc, base, x, bo, gain, beta, offs, out):
         spark = held.tile([C, 2], BF16, name="spark")
         nc.gpsimd.memset(spark[:], 1.0)
 
-        x_sb = held.tile([C, LEAD + N], F32, name="x_sb")
+        x_sb = held.tile([C, LEAD + N], F32, name="x_sb", tag="x_then_beta")
         offsets = held.tile([C, N // 16], U16, name="offsets")
         window = held.tile([C, S], F32, name="window")
         gain_sb = held.tile([C, 1], F32, name="gain_sb")
@@ -78,9 +78,6 @@ def tile_p2pdecoderlayer_kernel(tc, base, x, bo, gain, beta, offs, out):
                 start=True,
                 stop=True,
             )
-
-        beta_wide = held.tile([C, N], F32, name="beta_wide")
-        nc.vector.tensor_copy(beta_wide[:], beta_sb[:].to_broadcast([C, N]))
 
         sq = held.tile([C, N], F32, name="sq")
         gained = held.tile([C, N], F32, name="gained")
@@ -165,6 +162,8 @@ def tile_p2pdecoderlayer_kernel(tc, base, x, bo, gain, beta, offs, out):
         normalised_by_token(by_token)
         squared_and_gained(second_piece, centred(second_piece))
         squared_and_gained(last_piece, centred(last_piece))
+        beta_wide = held.tile([C, N], F32, name="beta_wide", tag="x_then_beta")
+        nc.vector.tensor_copy(beta_wide[:], beta_sb[:].to_broadcast([C, N]))
         normalised(first_piece * PIECE, (first_piece + 1) * PIECE)
         normalised(second_piece * PIECE, (second_piece + 1) * PIECE)
         turned_back()

@@ -36,12 +36,12 @@ def tile_p2pdecoderlayer_kernel(tc, base, x, bo, gain, beta, offs, out):
         spark = held.tile([C, 2], BF16, name="spark")
         nc.gpsimd.memset(spark[:], 1.0)
 
-        x_sb = held.tile([C, LEAD + N], F32, name="x_sb", tag="x_then_beta")
+        x_sb = held.tile([C, LEAD + N], F32, name="x_sb")
         offsets = held.tile([C, N // 16], U16, name="offsets")
         window = held.tile([C, S], F32, name="window")
         gain_sb = held.tile([C, 1], F32, name="gain_sb")
         beta_sb = held.tile([C, 1], F32, name="beta_sb")
-        for first, end in ((0, PIECE), (PIECE, 2 * PIECE), (2 * PIECE, N)):
+        for first, end in ((0, PIECE), (PIECE, N)):
             nc.sync.dma_start(x_sb[:, LEAD + first : LEAD + end], x[:, first:end])
         nc.sync.dma_start(offsets[:], offs)
         nc.sync.dma_start(window[:], base)
@@ -85,7 +85,7 @@ def tile_p2pdecoderlayer_kernel(tc, base, x, bo, gain, beta, offs, out):
         scaled = held.tile([C, N], F32, name="scaled")
         bo_centred = held.tile([C, 1], F32, name="bo_centred")
 
-        r = held.tile([C, PIECE], F32, name="r")
+        r = held.tile([C, PIECE], F32, name="r", tag="r_then_beta")
         stats = held.tile([C, BLOCKS, 6], F32, name="stats")
         moments = held.tile([C, BLOCKS, 2], F32, name="moments")
         rstd_token = held.tile([C, BLOCKS], F32, name="rstd_token")
@@ -162,7 +162,7 @@ def tile_p2pdecoderlayer_kernel(tc, base, x, bo, gain, beta, offs, out):
         normalised_by_token(by_token)
         squared_and_gained(second_piece, centred(second_piece))
         squared_and_gained(last_piece, centred(last_piece))
-        beta_wide = held.tile([C, N], F32, name="beta_wide", tag="x_then_beta")
+        beta_wide = held.tile([C, N], F32, name="beta_wide", tag="r_then_beta")
         nc.vector.tensor_copy(beta_wide[:], beta_sb[:].to_broadcast([C, N]))
         normalised(first_piece * PIECE, (first_piece + 1) * PIECE)
         normalised(second_piece * PIECE, (second_piece + 1) * PIECE)

@@ -18,7 +18,7 @@ BYTES = 4 * (C * S + C * (S - N) + C * N + 3 * C) + 2 * N
 PIECE = 256
 PIECES = N // PIECE
 LEAD = 8
-TURNED = 1
+TURNED = PIECES - 1
 BLOCK = 128
 BLOCKS = PIECE // BLOCK
 WARM_UP = 4
@@ -156,19 +156,20 @@ def tile_p2pdecoderlayer_kernel(tc, base, x, bo, gain, beta, offs, out):
             )
 
         first_piece, second_piece, last_piece = [p for p in range(PIECES) if p != TURNED]
-        x_centred = centred(first_piece)
+        first_centred = centred(first_piece)
+        second_centred = centred(second_piece)
         by_token = turned()
-        squared_and_gained(first_piece, x_centred)
+        squared_and_gained(first_piece, first_centred)
         normalised_by_token(by_token)
-        squared_and_gained(second_piece, centred(second_piece))
+        squared_and_gained(second_piece, second_centred)
         squared_and_gained(last_piece, centred(last_piece))
         beta_wide = held.tile([C, N], F32, name="beta_wide", tag="r_then_beta")
         nc.vector.tensor_copy(beta_wide[:], beta_sb[:].to_broadcast([C, N]))
         normalised(first_piece * PIECE, (first_piece + 1) * PIECE)
         normalised(second_piece * PIECE, (second_piece + 1) * PIECE)
         turned_back()
-        normalised(N - PIECE, N - PIECE // 2)
-        normalised(N - PIECE // 2, N)
+        normalised(last_piece * PIECE, last_piece * PIECE + PIECE // 2)
+        normalised(last_piece * PIECE + PIECE // 2, (last_piece + 1) * PIECE)
 
         nc.vector.tensor_tensor(window[:].indirect(offsets[:]), scaled[:], beta_wide[:], ALU.add)
         nc.sync.dma_start(out, window[:])

import concourse.masks as masks
import concourse.mybir as mybir

F32 = mybir.dt.float32
BF16 = mybir.dt.bfloat16
U16 = mybir.dt.uint16
ALU = mybir.AluOpType
ACT = mybir.ActivationFunctionType

C = 128
S = 4096
N = 1024
EPS = 1e-5

FLOPS = 9 * C * N
BYTES = 4 * (C * S + C * (S - N) + C * N + 3 * C) + 2 * N

PIECE = 256
PIECES = N // PIECE
LEAD = 8
TURNED = PIECES - 1
BLOCK = 128
BLOCKS = PIECE // BLOCK
WARM_UP = 4
BANK = 512


def tile_p2pdecoderlayer_kernel(tc, base, x, bo, gain, beta, offs, out):
    nc = tc.nc
    with (
        tc.tile_pool(name="held", bufs=1) as held,
        tc.psum_pool(name="psum_centred", bufs=PIECES - 1) as psum_centred,
        tc.psum_pool(name="psum_turned", bufs=1) as psum_turned,
        tc.psum_pool(name="psum_other", bufs=4) as psum_other,
    ):
        spark = held.tile([C, 2], BF16, name="spark")
        nc.gpsimd.memset(spark[:], 1.0)

        x_sb = held.tile([C, LEAD + N], F32, name="x_sb")
        offsets = held.tile([C, N // 16], U16, name="offsets")
        window = held.tile([C, S], F32, name="window")
        gain_sb = held.tile([C, 1], F32, name="gain_sb")
        beta_sb = held.tile([C, 1], F32, name="beta_sb")
        for first, end in ((0, PIECE), (PIECE, N)):
            nc.sync.dma_start(x_sb[:, LEAD + first : LEAD + end], x[:, first:end])
        nc.sync.dma_start(offsets[:], offs)
        nc.sync.dma_start(window[:], base)
        nc.scalar.dma_start(x_sb[:, LEAD - 1 : LEAD], bo)
        nc.scalar.dma_start(gain_sb[:], gain)
        nc.scalar.dma_start(beta_sb[:], beta)

        centre = held.tile([C, C], F32, name="centre")
        nc.gpsimd.memset(centre[:], -1.0 / C)
        nc.gpsimd.affine_select(
            out=centre[:],
            in_=centre[:],
            compare_op=ALU.not_equal,
            fill=1.0 - 1.0 / C,
            base=0,
            pattern=[[-1, C]],
            channel_multiplier=1,
        )
        identity = held.tile([C, C], F32, name="identity")
        masks.make_identity(nc, identity[:])
        average = held.tile([C, C], F32, name="average")
        nc.gpsimd.memset(average[:], 1.0 / C)
        eps_sb = held.tile([C, 1], F32, name="eps_sb")
        nc.vector.memset(eps_sb[:], EPS)

        table_warm = held.tile([C, 1], F32, name="table_warm")
        nc.scalar.activation(table_warm[:], eps_sb[:], ACT.Abs_reciprocal_sqrt)
        clock_warm = psum_other.tile([C, BANK], F32, name="clock_warm", tag="other")
        for repeat in range(WARM_UP):
            nc.tensor.matmul(
                clock_warm[:],
                spark[:, 0:1].to_broadcast([C, C]),
                spark[:, 0:1].to_broadcast([C, BANK]),
                start=True,
                stop=True,
            )

        sq = held.tile([C, N], F32, name="sq")
        gained = held.tile([C, N], F32, name="gained")
        rstd = held.tile([C, N], F32, name="rstd")
        scaled = held.tile([C, N], F32, name="scaled")
        bo_centred = held.tile([C, 1], F32, name="bo_centred")

        r = held.tile([C, PIECE], F32, name="r", tag="r_then_beta")
        stats = held.tile([C, BLOCKS, 6], F32, name="stats")
        moments = held.tile([C, BLOCKS, 2], F32, name="moments")
        rstd_token = held.tile([C, BLOCKS], F32, name="rstd_token")
        normal = held.tile([C, PIECE], F32, name="normal")
        blocks = [slice(b * BLOCK, (b + 1) * BLOCK) for b in range(BLOCKS)]

        def centred(p):
            extra = 1 if p == 0 else 0
            product = psum_centred.tile([C, extra + PIECE], F32, name="product")
            nc.tensor.matmul(
                product[:],
                centre[:],
                x_sb[:, LEAD + p * PIECE - extra : LEAD + (p + 1) * PIECE],
                start=True,
                stop=True,
            )
            if p == 0:
                nc.vector.tensor_copy(bo_centred[:], product[:, 0:1])
            return product[:, extra:]

        def squared_and_gained(p, x_centred):
            cols = slice(p * PIECE, (p + 1) * PIECE)
            nc.scalar.activation(sq[:, cols], x_centred, ACT.Square, bias=bo_centred[:])
            nc.vector.tensor_scalar(
                gained[:, cols], x_centred, bo_centred[:], gain_sb[:], ALU.add, ALU.mult
            )

        def normalised(first, end):
            cols = slice(first, end)
            var_p = psum_other.tile([C, end - first], F32, name="var_p", tag="other")
            nc.tensor.matmul(var_p[:], average[:], sq[:, cols], start=True, stop=True)
            nc.scalar.activation(rstd[:, cols], var_p[:], ACT.Abs_reciprocal_sqrt, bias=eps_sb[:])
            nc.vector.tensor_tensor(scaled[:, cols], gained[:, cols], rstd[:, cols], ALU.mult)

        def turned():
            nc.scalar.activation(
                r[:],
                x_sb[:, LEAD + TURNED * PIECE : LEAD + (TURNED + 1) * PIECE],
                ACT.Identity,
                bias=x_sb[:, LEAD - 1 : LEAD],
            )
            by_token = psum_turned.tile([C, PIECE], F32, name="by_token", tag="turned")
            for block in blocks:
                nc.tensor.transpose(by_token[:, block], r[:, block], identity[:])
            return by_token

        def normalised_by_token(by_token):
            for b, block in enumerate(blocks):
                nc.vector.bn_stats(stats[:, b, :], by_token[:, block])
                nc.vector.bn_aggr(moments[:, b, :], stats[:, b, :])
            nc.scalar.activation(rstd_token[:], moments[:, :, 1], ACT.Abs_reciprocal_sqrt, bias=eps_sb[:])
            for b, block in enumerate(blocks):
                nc.vector.tensor_scalar(
                    normal[:, block],
                    by_token[:, block],
                    moments[:, b, 0:1],
                    rstd_token[:, b : b + 1],
                    ALU.subtract,
                    ALU.mult,
                )

        def turned_back():
            by_channel = psum_turned.tile([C, PIECE], F32, name="by_channel", tag="turned")
            for block in blocks:
                nc.tensor.transpose(by_channel[:, block], normal[:, block], identity[:])
            nc.scalar.activation(
                scaled[:, TURNED * PIECE : (TURNED + 1) * PIECE], by_channel[:], ACT.Identity, scale=gain_sb[:]
            )

        first_piece, second_piece, last_piece = [p for p in range(PIECES) if p != TURNED]
        first_centred = centred(first_piece)
        second_centred = centred(second_piece)
        by_token = turned()
        squared_and_gained(first_piece, first_centred)
        normalised_by_token(by_token)
        squared_and_gained(second_piece, second_centred)
        squared_and_gained(last_piece, centred(last_piece))
        beta_wide = held.tile([C, N], F32, name="beta_wide", tag="r_then_beta")
        nc.vector.tensor_copy(beta_wide[:], beta_sb[:].to_broadcast([C, N]))
        normalised(first_piece * PIECE, (first_piece + 1) * PIECE)
        normalised(second_piece * PIECE, (second_piece + 1) * PIECE)
        turned_back()
        normalised(last_piece * PIECE, last_piece * PIECE + PIECE // 2)
        normalised(last_piece * PIECE + PIECE // 2, (last_piece + 1) * PIECE)

        nc.vector.tensor_tensor(window[:].indirect(offsets[:]), scaled[:], beta_wide[:], ALU.add)
        nc.sync.dma_start(out, window[:])
